import numpy as np
import ml_dtypes


def mxq(x, axis, fmt="e4m3"):
    dtype, down = {"e4m3": (ml_dtypes.float8_e4m3fn, 7), "e5m2": (ml_dtypes.float8_e5m2, 14)}[fmt]
    v = np.moveaxis(np.asarray(x, np.float32).astype(ml_dtypes.bfloat16).astype(np.float64), axis, -1)
    blocks = v.reshape(v.shape[:-1] + (-1, 32))
    amax = np.abs(blocks).max(-1, keepdims=True)
    byte = np.maximum(np.where(amax > 0, np.frexp(amax)[1] - 1 + 127, 0) - down, 1)
    scale = np.exp2(byte - 127.0)
    codes = (blocks / scale).astype(np.float32).astype(dtype).astype(np.float64)
    return np.moveaxis((codes * scale).reshape(v.shape), -1, axis)


WIDE = False


def mx_kscale(k):
    if not WIDE:
        return np.ones(k)
    levels = np.array([10, -10, 5, -5, 0])
    a = np.random.permutation(np.resize(levels, k // 512 * 4)).reshape(k // 512, 4)
    idx = np.arange(k)
    return np.exp2(a[idx // 512, idx % 128 // 32])


BF16 = ml_dtypes.bfloat16


def bf(x):
    return np.asarray(x, np.float32).astype(BF16)


def f64(x):
    return np.asarray(x).astype(np.float64)


NA, NB, H = 4096, 1024, 1024


def sigmoid(v):
    return 1.0 / (1.0 + np.exp(-v))


def setup_inputs():
    s, t = mx_kscale(H), mx_kscale(H)
    return {"y_a": bf(np.random.standard_normal((NA, H)) * 0.25 / t),
            "y_b": bf(np.random.standard_normal((NB, H)) * s),
            "W": bf(np.random.standard_normal((H, H)) * 6.0 / H * t[:, None] / s[None, :]),
            "b": bf(np.random.standard_normal(H) * 5.0 / np.sqrt(H) * t)}


def reference(y_a, y_b, W, b):
    proj = (mxq(f64(y_b), 1, "e4m3") @ mxq(f64(W), 1, "e4m3").T) + f64(b)
    scores = mxq(f64(y_a), 1, "e4m3") @ mxq(proj, 1, "e4m3").T
    s = np.sum(sigmoid(scores), axis=1) / y_a.shape[1]
    return np.broadcast_to(s[:, None], y_a.shape).copy()

@@ -1,0 +1,223 @@
+from contextlib import ExitStack
+
+import concourse.mybir as mybir
+from concourse.masks import make_identity
+
+F32 = mybir.dt.float32
+BF16 = mybir.dt.bfloat16
+U32 = mybir.dt.uint32
+U8 = mybir.dt.uint8
+FP8X4 = mybir.dt.float8_e4m3fn_x4
+ACT = mybir.ActivationFunctionType
+ALU = mybir.AluOpType
+
+P = 128
+K = 1024
+UNIT = 512
+NA = 4096
+NB = 1024
+GROUPS = NA // UNIT
+
+FLOPS = 2 * NB * K * K + 2 * NA * NB * K
+
+
+def tile_miscore_t_kernel(tc, y_a, y_b, W, b, out):
+    nc = tc.nc
+    with ExitStack() as ctx:
+        ctx.enter_context(tc.manual_schedule())
+        const = ctx.enter_context(tc.tile_pool(name="const", bufs=1))
+        rawp = ctx.enter_context(tc.tile_pool(name="rawp", bufs=1))
+        grpp = ctx.enter_context(tc.tile_pool(name="grpp", bufs=3))
+        midp = ctx.enter_context(tc.tile_pool(name="midp", bufs=2))
+        keep = ctx.enter_context(tc.tile_pool(name="keep", bufs=1))
+        yacp = ctx.enter_context(tc.tile_pool(name="yacp", bufs=3))
+        outp = ctx.enter_context(tc.tile_pool(name="outp", bufs=3))
+        scrp = ctx.enter_context(tc.tile_pool(name="scrp", bufs=2))
+        psum = ctx.enter_context(tc.psum_pool(name="psum", bufs=4))
+
+        ident = const.tile([P, P], F32, name="ident")
+        make_identity(nc, ident[:])
+        b_raw = const.tile([P, 8], BF16, name="b_raw")
+        with nc.allow_non_contiguous_dma(reason="bias: 512 pieces of two elements, once"):
+            nc.scalar.dma_start(
+                out=b_raw[:].rearrange("p (a e) -> p a e", e=2),
+                in_=b.rearrange("(a p e) -> p a e", p=P, e=2),
+            )
+        bias = const.tile([P, 8], F32, name="bias")
+        warm = const.tile([P, 8], F32, name="warm")
+        nc.vector.memset(warm[:, 0:1], 0.0)
+        nc.scalar.activation(out=warm[:, 1:2], in_=warm[:, 0:1], func=ACT.Sigmoid)
+
+        ya_v = y_a.rearrange("(g p r) k -> g p r k", p=P, r=4)
+        yb_v = y_b.rearrange("(g p r) k -> g p r k", p=P, r=4)
+        w_v = W.rearrange("(g u p e) k -> g u p e k", u=2, p=P, e=2)
+
+        def load(name, halves):
+            raw = rawp.tile([P, 4 * K], BF16, name=name)
+            n = len(halves)
+            for i, src in enumerate(halves):
+                w = 4 * K // n
+                nc.sync.dma_start(
+                    out=raw[:, i * w : (i + 1) * w].rearrange("p (r k) -> p r k", k=K), in_=src
+                )
+            return raw
+
+        raw_yb = [None, None]
+        raw_w = [None, None]
+        raw_yb[0] = load("raw_yb0", [yb_v[0][:, 0:2, :], yb_v[0][:, 2:4, :]])
+        raw_w[0] = load("raw_w0", [w_v[0][0], w_v[0][1]])
+        raw_w[1] = load("raw_w1", [w_v[1][0], w_v[1][1]])
+        raw_yb[1] = load("raw_yb1", [yb_v[1][:, 0:2, :], yb_v[1][:, 2:4, :]])
+        raw_ya = [load("raw_ya%d" % g, [ya_v[g]]) for g in range(GROUPS)]
+
+        nc.vector.tensor_copy(out=bias[:], in_=b_raw[:])
+
+        def copy_on(which, dst, src):
+            if which == "S":
+                nc.scalar.copy(out=dst, in_=src)
+            else:
+                nc.vector.tensor_copy(out=dst, in_=src)
+
+        def transposes(raw):
+            words = raw[:].bitcast(F32)
+            banks = []
+            for t in range(4):
+                xt = psum.tile([P, 4, P], F32, name="xt", tag="tp")
+                for c in range(4):
+                    lo = t * (K // 2) + c * P
+                    nc.tensor.transpose(xt[:, c, :], words[:, lo : lo + P], ident[:])
+                banks.append(xt)
+            grp = grpp.tile([P, 4 * K], BF16, name="grp", align_bytes=64)
+            return banks, grp
+
+        def evacuate(which, banks, grp, t):
+            gw = grp[:].bitcast(F32).rearrange("p (g c u) -> p g c u", g=2, u=2)
+            copy_on(
+                which,
+                gw[:, :, t * P : (t + 1) * P, :],
+                banks[t][:].rearrange("p (g u) i -> p g i u", g=2),
+            )
+
+        def quantise(grp, op):
+            nc.vector.quantize_mx(out=op[0][:].bitcast(FP8X4), scales=op[1][:], in_=grp[:])
+
+        def prepare(raw, op, engines):
+            banks, grp = transposes(raw)
+            for t in range(4):
+                evacuate(engines[t], banks, grp, t)
+            quantise(grp, op)
+
+        def operand(pool, name):
+            codes = pool.tile([P, 2 * UNIT], U32, name=name + "_c", align_bytes=64)
+            scales = pool.tile([P, 2 * UNIT], U8, name=name + "_s", align_bytes=64)
+            return codes, scales
+
+        def mx_group(acc, lc, ls, m0, rc, rs):
+            for gk in range(2):
+                ml = slice(gk * UNIT + m0, gk * UNIT + m0 + P)
+                nl = slice(gk * UNIT, (gk + 1) * UNIT)
+                nc.tensor.matmul_mx(
+                    out=acc[:],
+                    lhsT=lc[:, ml].bitcast(FP8X4),
+                    lhsT_scale=ls[:, ml],
+                    rhs=rc[:, nl].bitcast(FP8X4),
+                    rhs_scale=rs[:, nl],
+                    start=(gk == 0),
+                    stop=(gk == 1),
+                )
+
+        yb_op = [operand(keep, "yb%d" % h) for h in range(2)]
+        w_op = [operand(keep, "w%d" % g) for g in range(2)]
+        pj_op = [operand(keep, "pj%d" % h) for h in range(2)]
+
+        def stage1(go, h, engines):
+            mid = midp.tile([P, 4 * UNIT], BF16, name="mid")
+            for t in range(4):
+                acc = psum.tile([P, UNIT], F32, name="acc", tag="mm")
+                mx_group(acc, w_op[go][0], w_op[go][1], t * P, yb_op[h][0], yb_op[h][1])
+                col = go * 4 + t
+                dst = mid[:, t * UNIT : (t + 1) * UNIT]
+                if engines[t] == "S":
+                    nc.scalar.activation(
+                        out=dst, in_=acc[:], func=ACT.Identity, bias=bias[:, col : col + 1], scale=1.0
+                    )
+                else:
+                    nc.vector.tensor_scalar(
+                        out=dst, in0=acc[:], scalar1=bias[:, col : col + 1], scalar2=None, op0=ALU.add
+                    )
+            pgrp = midp.tile([P, 4 * UNIT], BF16, name="pgrp", align_bytes=64)
+            nc.vector.tensor_copy(
+                out=pgrp[:].rearrange("p (c i t) -> p c t i", i=4, t=4),
+                in_=mid[:].rearrange("p (t c i) -> p c t i", t=4, i=4),
+            )
+            nl = slice(go * UNIT, (go + 1) * UNIT)
+            nc.vector.quantize_mx(
+                out=pj_op[h][0][:, nl].bitcast(FP8X4), scales=pj_op[h][1][:, nl], in_=pgrp[:]
+            )
+
+        out_v = out.rearrange("(g p r) (c k) -> g c p r k", p=P, r=4, c=2)
+
+        def scores(g, op, sums, r, h):
+            acc = psum.tile([P, UNIT], F32, name="acc", tag="mm")
+            mx_group(acc, op[0], op[1], r * P, pj_op[h][0], pj_op[h][1])
+            scr = scrp.tile([P, UNIT], F32, name="scr")
+            col = 2 * r + h
+            nc.scalar.activation(
+                out=scr[:], in_=acc[:], func=ACT.Sigmoid, accum_out=sums[:, col : col + 1]
+            )
+
+        def finish(g, sums, ot, r):
+            nc.vector.tensor_scalar(
+                out=ot[:, r * UNIT : (r + 1) * UNIT],
+                in0=sums[:, 2 * r : 2 * r + 1].to_broadcast([P, UNIT]),
+                scalar1=sums[:, 2 * r + 1 : 2 * r + 2],
+                scalar2=1.0 / K,
+                op0=ALU.add,
+                op1=ALU.mult,
+            )
+            for c in range(2):
+                nc.sync.dma_start(out=out_v[g][c][:, r, :], in_=ot[:, r * UNIT : (r + 1) * UNIT])
+
+        prepare(raw_yb[0], yb_op[0], "SVSS")
+        prepare(raw_w[0], w_op[0], "SVSS")
+        prepare(raw_w[1], w_op[1], "SVSS")
+        stage1(0, 0, "SSSV")
+        prepare(raw_yb[1], yb_op[1], "SVSS")
+        stage1(1, 0, "SSSV")
+        ya_op = operand(yacp, "ya")
+        prepare(raw_ya[0], ya_op, "SVSV")
+        stage1(0, 1, "SSSV")
+        stage1(1, 1, "SSSV")
+        late = None
+        for g in range(GROUPS):
+            sums = scrp.tile([P, 8], F32, name="sums", bufs=3)
+            ot = outp.tile([P, 4 * UNIT], F32, name="ot")
+            more = g + 1 < GROUPS
+            if more:
+                next_op = operand(yacp, "ya")
+                banks, grp = transposes(raw_ya[g + 1])
+                evacuate("V", banks, grp, 0)
+            if late is not None:
+                finish(*late)
+            if more:
+                for t in range(1, 4):
+                    evacuate("V", banks, grp, t)
+            if g == 0:
+                for h in range(2):
+                    for r in range(4):
+                        scores(g, ya_op, sums, r, h)
+                quantise(grp, next_op)
+                for r in range(3):
+                    finish(g, sums, ot, r)
+            else:
+                for r in range(4):
+                    for h in range(2):
+                        scores(g, ya_op, sums, r, h)
+                    if r < 3:
+                        finish(g, sums, ot, r)
+                    if r == 0 and more:
+                        quantise(grp, next_op)
+            late = (g, sums, ot, 3)
+            if more:
+                ya_op = next_op
+        finish(*late)

@@ -167,7 +167,8 @@ def tile_miscore_t_kernel(tc, y_a, y_b, W, b, out):
             )
 
         def finish(g, sums, ot, r):
-            nc.vector.tensor_scalar(
+            filler = nc.vector if g == GROUPS - 1 else nc.gpsimd
+            filler.tensor_scalar(
                 out=ot[:, r * UNIT : (r + 1) * UNIT],
                 in0=sums[:, 2 * r : 2 * r + 1].to_broadcast([P, UNIT]),
                 scalar1=sums[:, 2 * r + 1 : 2 * r + 2],
@@ -181,13 +182,13 @@ def tile_miscore_t_kernel(tc, y_a, y_b, W, b, out):
         prepare(raw_yb[0], yb_op[0], "SVSS")
         prepare(raw_w[0], w_op[0], "SVSS")
         prepare(raw_w[1], w_op[1], "SVSS")
-        stage1(0, 0, "SSSV")
+        stage1(0, 0, "SSSS")
         prepare(raw_yb[1], yb_op[1], "SVSS")
-        stage1(1, 0, "SSSV")
+        stage1(1, 0, "SSSS")
         ya_op = operand(yacp, "ya")
         prepare(raw_ya[0], ya_op, "SVSV")
-        stage1(0, 1, "SSSV")
-        stage1(1, 1, "SSSV")
+        stage1(0, 1, "SSSS")
+        stage1(1, 1, "SSSS")
         late = None
         for g in range(GROUPS):
             sums = scrp.tile([P, 8], F32, name="sums", bufs=3)

@@ -17,6 +17,7 @@ UNIT = 512
 NA = 4096
 NB = 1024
 GROUPS = NA // UNIT
+WARM = 8
 
 FLOPS = 2 * NB * K * K + 2 * NA * NB * K
 
@@ -48,6 +49,18 @@ def tile_miscore_t_kernel(tc, y_a, y_b, W, b, out):
         nc.vector.memset(warm[:, 0:1], 0.0)
         nc.scalar.activation(out=warm[:, 1:2], in_=warm[:, 0:1], func=ACT.Sigmoid)
 
+        zl = const.tile([P, P], BF16, name="zl")
+        zr = const.tile([P, UNIT], BF16, name="zr")
+        nc.vector.memset(zl[:], 0.0)
+        nc.vector.memset(zr[:], 0.0)
+
+        def idle_matmuls(n):
+            for i in range(n):
+                junk = psum.tile([P, UNIT], F32, name="junk", tag="mm")
+                nc.tensor.matmul(out=junk[:], lhsT=zl[:], rhs=zr[:], start=True, stop=True)
+
+        idle_matmuls(WARM)
+
         ya_v = y_a.rearrange("(g p r) k -> g p r k", p=P, r=4)
         yb_v = y_b.rearrange("(g p r) k -> g p r k", p=P, r=4)
         w_v = W.rearrange("(g u p e) k -> g u p e k", u=2, p=P, e=2)
@@ -78,7 +91,7 @@ def tile_miscore_t_kernel(tc, y_a, y_b, W, b, out):
             else:
                 nc.vector.tensor_copy(out=dst, in_=src)
 
-        def transposes(raw):
+        def transposes(raw, fill=False):
             words = raw[:].bitcast(F32)
             banks = []
             for t in range(4):
@@ -87,6 +100,8 @@ def tile_miscore_t_kernel(tc, y_a, y_b, W, b, out):
                     lo = t * (K // 2) + c * P
                     nc.tensor.transpose(xt[:, c, :], words[:, lo : lo + P], ident[:])
                 banks.append(xt)
+                if fill and t % 2 == 1:
+                    idle_matmuls(1)
             grp = grpp.tile([P, 4 * K], BF16, name="grp", align_bytes=64)
             return banks, grp
 
@@ -101,8 +116,8 @@ def tile_miscore_t_kernel(tc, y_a, y_b, W, b, out):
         def quantise(grp, op):
             nc.vector.quantize_mx(out=op[0][:].bitcast(FP8X4), scales=op[1][:], in_=grp[:])
 
-        def prepare(raw, op, engines):
-            banks, grp = transposes(raw)
+        def prepare(raw, op, engines, fill=False):
+            banks, grp = transposes(raw, fill)
             for t in range(4):
                 evacuate(engines[t], banks, grp, t)
             quantise(grp, op)
@@ -179,9 +194,9 @@ def tile_miscore_t_kernel(tc, y_a, y_b, W, b, out):
             for c in range(2):
                 nc.sync.dma_start(out=out_v[g][c][:, r, :], in_=ot[:, r * UNIT : (r + 1) * UNIT])
 
-        prepare(raw_yb[0], yb_op[0], "SVSS")
-        prepare(raw_w[0], w_op[0], "SVSS")
-        prepare(raw_w[1], w_op[1], "SVSS")
+        prepare(raw_yb[0], yb_op[0], "SVSS", True)
+        prepare(raw_w[0], w_op[0], "SVSS", True)
+        prepare(raw_w[1], w_op[1], "SVSS", True)
         stage1(0, 0, "SSSS")
         prepare(raw_yb[1], yb_op[1], "SVSS")
         stage1(1, 0, "SSSS")

@@ -18,6 +18,7 @@ NA = 4096
 NB = 1024
 GROUPS = NA // UNIT
 WARM = 8
+AHEAD = 4
 
 FLOPS = 2 * NB * K * K + 2 * NA * NB * K
 
@@ -36,23 +37,18 @@ def tile_miscore_t_kernel(tc, y_a, y_b, W, b, out):
         scrp = ctx.enter_context(tc.tile_pool(name="scrp", bufs=2))
         psum = ctx.enter_context(tc.psum_pool(name="psum", bufs=4))
 
+        b_rows = const.tile([P, 2 * P], BF16, name="b_rows")
+        nc.vector.memset(b_rows[:], 0.0)
+        nc.scalar.dma_start(out=b_rows[0:4, :], in_=b.rearrange("(a w) -> a w", w=2 * P))
         ident = const.tile([P, P], F32, name="ident")
         make_identity(nc, ident[:])
-        b_raw = const.tile([P, 8], BF16, name="b_raw")
-        with nc.allow_non_contiguous_dma(reason="bias: 512 pieces of two elements, once"):
-            nc.scalar.dma_start(
-                out=b_raw[:].rearrange("p (a e) -> p a e", e=2),
-                in_=b.rearrange("(a p e) -> p a e", p=P, e=2),
-            )
-        bias = const.tile([P, 8], F32, name="bias")
-        warm = const.tile([P, 8], F32, name="warm")
-        nc.vector.memset(warm[:, 0:1], 0.0)
-        nc.scalar.activation(out=warm[:, 1:2], in_=warm[:, 0:1], func=ACT.Sigmoid)
-
         zl = const.tile([P, P], BF16, name="zl")
         zr = const.tile([P, UNIT], BF16, name="zr")
         nc.vector.memset(zl[:], 0.0)
         nc.vector.memset(zr[:], 0.0)
+        warm = const.tile([P, 8], F32, name="warm")
+        nc.vector.memset(warm[:, 0:1], 0.0)
+        nc.scalar.activation(out=warm[:, 1:2], in_=warm[:, 0:1], func=ACT.Sigmoid)
 
         def idle_matmuls(n):
             for i in range(n):
@@ -65,31 +61,32 @@ def tile_miscore_t_kernel(tc, y_a, y_b, W, b, out):
         yb_v = y_b.rearrange("(g p r) k -> g p r k", p=P, r=4)
         w_v = W.rearrange("(g u p e) k -> g u p e k", u=2, p=P, e=2)
 
-        def load(name, halves):
+        def load(name, pieces):
             raw = rawp.tile([P, 4 * K], BF16, name=name)
-            n = len(halves)
-            for i, src in enumerate(halves):
-                w = 4 * K // n
+            w = 4 * K // len(pieces)
+            for i, src in enumerate(pieces):
                 nc.sync.dma_start(
                     out=raw[:, i * w : (i + 1) * w].rearrange("p (r k) -> p r k", k=K), in_=src
                 )
             return raw
 
-        raw_yb = [None, None]
-        raw_w = [None, None]
-        raw_yb[0] = load("raw_yb0", [yb_v[0][:, 0:2, :], yb_v[0][:, 2:4, :]])
-        raw_w[0] = load("raw_w0", [w_v[0][0], w_v[0][1]])
-        raw_w[1] = load("raw_w1", [w_v[1][0], w_v[1][1]])
-        raw_yb[1] = load("raw_yb1", [yb_v[1][:, 0:2, :], yb_v[1][:, 2:4, :]])
+        raw_yb0 = load("raw_yb0", [yb_v[0][:, 0:2, :], yb_v[0][:, 2:4, :]])
+        raw_w0 = load("raw_w0", [w_v[0][0], w_v[0][1]])
+        raw_w1 = load("raw_w1", [w_v[1][0], w_v[1][1]])
+        raw_yb1 = load("raw_yb1", [yb_v[1][:, 0:2, :], yb_v[1][:, 2:4, :]])
         raw_ya = [load("raw_ya%d" % g, [ya_v[g]]) for g in range(GROUPS)]
 
-        nc.vector.tensor_copy(out=bias[:], in_=b_raw[:])
+        b_t = psum.tile([P, 4, P], F32, name="b_t", tag="tp")
+        nc.tensor.transpose(b_t[:, 0, :], b_rows[:].bitcast(F32), ident[:])
+        b_words = const.tile([P, 4], F32, name="b_words")
+        nc.vector.tensor_copy(out=b_words[:], in_=b_t[:, 0, 0:4])
+        bias = const.tile([P, 8], F32, name="bias")
+        nc.vector.tensor_copy(out=bias[:], in_=b_words[:].bitcast(BF16))
 
-        def copy_on(which, dst, src):
-            if which == "S":
-                nc.scalar.copy(out=dst, in_=src)
-            else:
-                nc.vector.tensor_copy(out=dst, in_=src)
+        def operand(pool, name):
+            codes = pool.tile([P, 2 * UNIT], U32, name=name + "_c", align_bytes=64)
+            scales = pool.tile([P, 2 * UNIT], U8, name=name + "_s", align_bytes=64)
+            return codes, scales
 
         def transposes(raw, fill=False):
             words = raw[:].bitcast(F32)
@@ -105,38 +102,47 @@ def tile_miscore_t_kernel(tc, y_a, y_b, W, b, out):
             grp = grpp.tile([P, 4 * K], BF16, name="grp", align_bytes=64)
             return banks, grp
 
-        def evacuate(which, banks, grp, t):
-            gw = grp[:].bitcast(F32).rearrange("p (g c u) -> p g c u", g=2, u=2)
-            copy_on(
-                which,
-                gw[:, :, t * P : (t + 1) * P, :],
-                banks[t][:].rearrange("p (g u) i -> p g i u", g=2),
+        def evacuate(which, banks, grp, t, moving):
+            gw = grp[:].bitcast(F32)
+            if moving:
+                dst = gw.rearrange("p (g c u) -> p g c u", g=2, u=2)[:, :, t * P : (t + 1) * P, :]
+            else:
+                dst = gw[:, t * UNIT : (t + 1) * UNIT].rearrange("p (g i u) -> p g i u", g=2, u=2)
+            src = banks[t][:].rearrange("p (g u) i -> p g i u", g=2)
+            if which == "S":
+                nc.scalar.copy(out=dst, in_=src)
+            else:
+                nc.vector.tensor_copy(out=dst, in_=src)
+
+        def quantise(grp, op, lo, hi):
+            nc.vector.quantize_mx(
+                out=op[0][:, lo:hi].bitcast(FP8X4), scales=op[1][:, lo:hi], in_=grp[:, 4 * lo : 4 * hi]
             )
 
-        def quantise(grp, op):
-            nc.vector.quantize_mx(out=op[0][:].bitcast(FP8X4), scales=op[1][:], in_=grp[:])
-
-        def prepare(raw, op, engines, fill=False):
+        def prepare(raw, op, engines, moving, halves, fill=False):
             banks, grp = transposes(raw, fill)
             for t in range(4):
-                evacuate(engines[t], banks, grp, t)
-            quantise(grp, op)
+                evacuate(engines[t], banks, grp, t, moving)
+                if halves and t % 2 == 1:
+                    a = t // 2
+                    if moving:
+                        for g in range(2):
+                            quantise(grp, op, g * UNIT + a * 2 * P, g * UNIT + (a + 1) * 2 * P)
+                    else:
+                        quantise(grp, op, a * UNIT, (a + 1) * UNIT)
+            if not halves:
+                quantise(grp, op, 0, 2 * UNIT)
 
-        def operand(pool, name):
-            codes = pool.tile([P, 2 * UNIT], U32, name=name + "_c", align_bytes=64)
-            scales = pool.tile([P, 2 * UNIT], U8, name=name + "_s", align_bytes=64)
-            return codes, scales
-
-        def mx_group(acc, lc, ls, m0, rc, rs):
+        def mx_group(acc, st_op, t, mv_op):
             for gk in range(2):
-                ml = slice(gk * UNIT + m0, gk * UNIT + m0 + P)
+                ml = slice(t * 2 * P + gk * P, t * 2 * P + (gk + 1) * P)
                 nl = slice(gk * UNIT, (gk + 1) * UNIT)
                 nc.tensor.matmul_mx(
                     out=acc[:],
-                    lhsT=lc[:, ml].bitcast(FP8X4),
-                    lhsT_scale=ls[:, ml],
-                    rhs=rc[:, nl].bitcast(FP8X4),
-                    rhs_scale=rs[:, nl],
+                    lhsT=st_op[0][:, ml].bitcast(FP8X4),
+                    lhsT_scale=st_op[1][:, ml],
+                    rhs=mv_op[0][:, nl].bitcast(FP8X4),
+                    rhs_scale=mv_op[1][:, nl],
                     start=(gk == 0),
                     stop=(gk == 1),
                 )
@@ -145,36 +151,35 @@ def tile_miscore_t_kernel(tc, y_a, y_b, W, b, out):
         w_op = [operand(keep, "w%d" % g) for g in range(2)]
         pj_op = [operand(keep, "pj%d" % h) for h in range(2)]
 
-        def stage1(go, h, engines):
+        def stage1(go, h):
             mid = midp.tile([P, 4 * UNIT], BF16, name="mid")
             for t in range(4):
                 acc = psum.tile([P, UNIT], F32, name="acc", tag="mm")
-                mx_group(acc, w_op[go][0], w_op[go][1], t * P, yb_op[h][0], yb_op[h][1])
+                mx_group(acc, w_op[go], t, yb_op[h])
                 col = go * 4 + t
-                dst = mid[:, t * UNIT : (t + 1) * UNIT]
-                if engines[t] == "S":
-                    nc.scalar.activation(
-                        out=dst, in_=acc[:], func=ACT.Identity, bias=bias[:, col : col + 1], scale=1.0
-                    )
-                else:
-                    nc.vector.tensor_scalar(
-                        out=dst, in0=acc[:], scalar1=bias[:, col : col + 1], scalar2=None, op0=ALU.add
-                    )
+                nc.scalar.activation(
+                    out=mid[:, t * UNIT : (t + 1) * UNIT],
+                    in_=acc[:],
+                    func=ACT.Identity,
+                    bias=bias[:, col : col + 1],
+                    scale=1.0,
+                )
             pgrp = midp.tile([P, 4 * UNIT], BF16, name="pgrp", align_bytes=64)
             nc.vector.tensor_copy(
                 out=pgrp[:].rearrange("p (c i t) -> p c t i", i=4, t=4),
                 in_=mid[:].rearrange("p (t c i) -> p c t i", t=4, i=4),
             )
-            nl = slice(go * UNIT, (go + 1) * UNIT)
             nc.vector.quantize_mx(
-                out=pj_op[h][0][:, nl].bitcast(FP8X4), scales=pj_op[h][1][:, nl], in_=pgrp[:]
+                out=pj_op[h][0][:, go * UNIT : (go + 1) * UNIT].bitcast(FP8X4),
+                scales=pj_op[h][1][:, go * UNIT : (go + 1) * UNIT],
+                in_=pgrp[:],
             )
 
         out_v = out.rearrange("(g p r) (c k) -> g c p r k", p=P, r=4, c=2)
 
-        def scores(g, op, sums, r, h):
+        def scores(op, sums, r, h):
             acc = psum.tile([P, UNIT], F32, name="acc", tag="mm")
-            mx_group(acc, op[0], op[1], r * P, pj_op[h][0], pj_op[h][1])
+            mx_group(acc, op, r, pj_op[h])
             scr = scrp.tile([P, UNIT], F32, name="scr")
             col = 2 * r + h
             nc.scalar.activation(
@@ -194,46 +199,34 @@ def tile_miscore_t_kernel(tc, y_a, y_b, W, b, out):
             for c in range(2):
                 nc.sync.dma_start(out=out_v[g][c][:, r, :], in_=ot[:, r * UNIT : (r + 1) * UNIT])
 
-        prepare(raw_yb[0], yb_op[0], "SVSS", True)
-        prepare(raw_w[0], w_op[0], "SVSS", True)
-        prepare(raw_w[1], w_op[1], "SVSS", True)
-        stage1(0, 0, "SSSS")
-        prepare(raw_yb[1], yb_op[1], "SVSS")
-        stage1(1, 0, "SSSS")
+        prepare(raw_yb0, yb_op[0], "SVSS", True, False, True)
+        prepare(raw_w0, w_op[0], "SVSS", False, True, True)
+        prepare(raw_w1, w_op[1], "SVSS", False, True, True)
+        stage1(0, 0)
+        prepare(raw_yb1, yb_op[1], "SVSS", True, True)
+        stage1(1, 0)
         ya_op = operand(yacp, "ya")
-        prepare(raw_ya[0], ya_op, "SVSV")
-        stage1(0, 1, "SSSS")
-        stage1(1, 1, "SSSS")
-        late = None
+        prepare(raw_ya[0], ya_op, "SVSV", False, False)
+        stage1(0, 1)
+        stage1(1, 1)
         for g in range(GROUPS):
             sums = scrp.tile([P, 8], F32, name="sums", bufs=3)
             ot = outp.tile([P, 4 * UNIT], F32, name="ot")
             more = g + 1 < GROUPS
-            if more:
-                next_op = operand(yacp, "ya")
-                banks, grp = transposes(raw_ya[g + 1])
-                evacuate("V", banks, grp, 0)
-            if late is not None:
-                finish(*late)
-            if more:
-                for t in range(1, 4):
-                    evacuate("V", banks, grp, t)
             if g == 0:
+                next_op = operand(yacp, "ya")
+                prepare(raw_ya[1], next_op, "VVVV", False, True)
                 for h in range(2):
                     for r in range(4):
-                        scores(g, ya_op, sums, r, h)
-                quantise(grp, next_op)
-                for r in range(3):
-                    finish(g, sums, ot, r)
+                        scores(ya_op, sums, r, h)
+                        if h == 1:
+                            finish(g, sums, ot, r)
             else:
                 for r in range(4):
+                    if more and r == 4 - AHEAD:
+                        next_op = operand(yacp, "ya")
+                        prepare(raw_ya[g + 1], next_op, "VVVV", False, True)
                     for h in range(2):
-                        scores(g, ya_op, sums, r, h)
-                    if r < 3:
-                        finish(g, sums, ot, r)
-                    if r == 0 and more:
-                        quantise(grp, next_op)
-            late = (g, sums, ot, 3)
-            if more:
-                ya_op = next_op
-        finish(*late)
+                        scores(ya_op, sums, r, h)
+                    finish(g, sums, ot, r)
+            ya_op = next_op

@@ -18,7 +18,6 @@ NA = 4096
 NB = 1024
 GROUPS = NA // UNIT
 WARM = 8
-AHEAD = 4
 
 FLOPS = 2 * NB * K * K + 2 * NA * NB * K
 
@@ -37,18 +36,23 @@ def tile_miscore_t_kernel(tc, y_a, y_b, W, b, out):
         scrp = ctx.enter_context(tc.tile_pool(name="scrp", bufs=2))
         psum = ctx.enter_context(tc.psum_pool(name="psum", bufs=4))
 
-        b_rows = const.tile([P, 2 * P], BF16, name="b_rows")
-        nc.vector.memset(b_rows[:], 0.0)
-        nc.scalar.dma_start(out=b_rows[0:4, :], in_=b.rearrange("(a w) -> a w", w=2 * P))
         ident = const.tile([P, P], F32, name="ident")
         make_identity(nc, ident[:])
+        b_raw = const.tile([P, 8], BF16, name="b_raw")
+        with nc.allow_non_contiguous_dma(reason="bias: 512 pieces of two elements, once"):
+            nc.scalar.dma_start(
+                out=b_raw[:].rearrange("p (a e) -> p a e", e=2),
+                in_=b.rearrange("(a p e) -> p a e", p=P, e=2),
+            )
+        bias = const.tile([P, 8], F32, name="bias")
+        warm = const.tile([P, 8], F32, name="warm")
+        nc.vector.memset(warm[:, 0:1], 0.0)
+        nc.scalar.activation(out=warm[:, 1:2], in_=warm[:, 0:1], func=ACT.Sigmoid)
+
         zl = const.tile([P, P], BF16, name="zl")
         zr = const.tile([P, UNIT], BF16, name="zr")
         nc.vector.memset(zl[:], 0.0)
         nc.vector.memset(zr[:], 0.0)
-        warm = const.tile([P, 8], F32, name="warm")
-        nc.vector.memset(warm[:, 0:1], 0.0)
-        nc.scalar.activation(out=warm[:, 1:2], in_=warm[:, 0:1], func=ACT.Sigmoid)
 
         def idle_matmuls(n):
             for i in range(n):
@@ -61,32 +65,29 @@ def tile_miscore_t_kernel(tc, y_a, y_b, W, b, out):
         yb_v = y_b.rearrange("(g p r) k -> g p r k", p=P, r=4)
         w_v = W.rearrange("(g u p e) k -> g u p e k", u=2, p=P, e=2)
 
-        def load(name, pieces):
+        def load(name, halves):
             raw = rawp.tile([P, 4 * K], BF16, name=name)
-            w = 4 * K // len(pieces)
-            for i, src in enumerate(pieces):
+            n = len(halves)
+            for i, src in enumerate(halves):
+                w = 4 * K // n
                 nc.sync.dma_start(
                     out=raw[:, i * w : (i + 1) * w].rearrange("p (r k) -> p r k", k=K), in_=src
                 )
             return raw
 
-        raw_yb0 = load("raw_yb0", [yb_v[0][:, 0:2, :], yb_v[0][:, 2:4, :]])
-        raw_w0 = load("raw_w0", [w_v[0][0], w_v[0][1]])
-        raw_w1 = load("raw_w1", [w_v[1][0], w_v[1][1]])
-        raw_yb1 = load("raw_yb1", [yb_v[1][:, 0:2, :], yb_v[1][:, 2:4, :]])
+        raw_yb = [None, None]
+        raw_w = [None, None]
+        raw_yb[0] = load("raw_yb0", [yb_v[0][:, 0:2, :], yb_v[0][:, 2:4, :]])
+        raw_w[0] = load("raw_w0", [w_v[0][0], w_v[0][1]])
+        raw_w[1] = load("raw_w1", [w_v[1][0], w_v[1][1]])
+        raw_yb[1] = load("raw_yb1", [yb_v[1][:, 0:2, :], yb_v[1][:, 2:4, :]])
         raw_ya = [load("raw_ya%d" % g, [ya_v[g]]) for g in range(GROUPS)]
 
-        b_t = psum.tile([P, 4, P], F32, name="b_t", tag="tp")
-        nc.tensor.transpose(b_t[:, 0, :], b_rows[:].bitcast(F32), ident[:])
-        b_words = const.tile([P, 4], F32, name="b_words")
-        nc.vector.tensor_copy(out=b_words[:], in_=b_t[:, 0, 0:4])
-        bias = const.tile([P, 8], F32, name="bias")
-        nc.vector.tensor_copy(out=bias[:], in_=b_words[:].bitcast(BF16))
-
-        def operand(pool, name):
-            codes = pool.tile([P, 2 * UNIT], U32, name=name + "_c", align_bytes=64)
-            scales = pool.tile([P, 2 * UNIT], U8, name=name + "_s", align_bytes=64)
-            return codes, scales
+        def copy_on(which, dst, src):
+            if which == "S":
+                nc.scalar.copy(out=dst, in_=src)
+            else:
+                nc.vector.tensor_copy(out=dst, in_=src)
 
         def transposes(raw, fill=False):
             words = raw[:].bitcast(F32)
@@ -102,47 +103,38 @@ def tile_miscore_t_kernel(tc, y_a, y_b, W, b, out):
             grp = grpp.tile([P, 4 * K], BF16, name="grp", align_bytes=64)
             return banks, grp
 
-        def evacuate(which, banks, grp, t, moving):
-            gw = grp[:].bitcast(F32)
-            if moving:
-                dst = gw.rearrange("p (g c u) -> p g c u", g=2, u=2)[:, :, t * P : (t + 1) * P, :]
-            else:
-                dst = gw[:, t * UNIT : (t + 1) * UNIT].rearrange("p (g i u) -> p g i u", g=2, u=2)
-            src = banks[t][:].rearrange("p (g u) i -> p g i u", g=2)
-            if which == "S":
-                nc.scalar.copy(out=dst, in_=src)
-            else:
-                nc.vector.tensor_copy(out=dst, in_=src)
-
-        def quantise(grp, op, lo, hi):
-            nc.vector.quantize_mx(
-                out=op[0][:, lo:hi].bitcast(FP8X4), scales=op[1][:, lo:hi], in_=grp[:, 4 * lo : 4 * hi]
+        def evacuate(which, banks, grp, t):
+            gw = grp[:].bitcast(F32).rearrange("p (g c u) -> p g c u", g=2, u=2)
+            copy_on(
+                which,
+                gw[:, :, t * P : (t + 1) * P, :],
+                banks[t][:].rearrange("p (g u) i -> p g i u", g=2),
             )
 
-        def prepare(raw, op, engines, moving, halves, fill=False):
+        def quantise(grp, op):
+            nc.vector.quantize_mx(out=op[0][:].bitcast(FP8X4), scales=op[1][:], in_=grp[:])
+
+        def prepare(raw, op, engines, fill=False):
             banks, grp = transposes(raw, fill)
             for t in range(4):
-                evacuate(engines[t], banks, grp, t, moving)
-                if halves and t % 2 == 1:
-                    a = t // 2
-                    if moving:
-                        for g in range(2):
-                            quantise(grp, op, g * UNIT + a * 2 * P, g * UNIT + (a + 1) * 2 * P)
-                    else:
-                        quantise(grp, op, a * UNIT, (a + 1) * UNIT)
-            if not halves:
-                quantise(grp, op, 0, 2 * UNIT)
+                evacuate(engines[t], banks, grp, t)
+            quantise(grp, op)
 
-        def mx_group(acc, st_op, t, mv_op):
+        def operand(pool, name):
+            codes = pool.tile([P, 2 * UNIT], U32, name=name + "_c", align_bytes=64)
+            scales = pool.tile([P, 2 * UNIT], U8, name=name + "_s", align_bytes=64)
+            return codes, scales
+
+        def mx_group(acc, lc, ls, m0, rc, rs):
             for gk in range(2):
-                ml = slice(t * 2 * P + gk * P, t * 2 * P + (gk + 1) * P)
+                ml = slice(gk * UNIT + m0, gk * UNIT + m0 + P)
                 nl = slice(gk * UNIT, (gk + 1) * UNIT)
                 nc.tensor.matmul_mx(
                     out=acc[:],
-                    lhsT=st_op[0][:, ml].bitcast(FP8X4),
-                    lhsT_scale=st_op[1][:, ml],
-                    rhs=mv_op[0][:, nl].bitcast(FP8X4),
-                    rhs_scale=mv_op[1][:, nl],
+                    lhsT=lc[:, ml].bitcast(FP8X4),
+                    lhsT_scale=ls[:, ml],
+                    rhs=rc[:, nl].bitcast(FP8X4),
+                    rhs_scale=rs[:, nl],
                     start=(gk == 0),
                     stop=(gk == 1),
                 )
@@ -151,35 +143,36 @@ def tile_miscore_t_kernel(tc, y_a, y_b, W, b, out):
         w_op = [operand(keep, "w%d" % g) for g in range(2)]
         pj_op = [operand(keep, "pj%d" % h) for h in range(2)]
 
-        def stage1(go, h):
+        def stage1(go, h, engines):
             mid = midp.tile([P, 4 * UNIT], BF16, name="mid")
             for t in range(4):
                 acc = psum.tile([P, UNIT], F32, name="acc", tag="mm")
-                mx_group(acc, w_op[go], t, yb_op[h])
+                mx_group(acc, w_op[go][0], w_op[go][1], t * P, yb_op[h][0], yb_op[h][1])
                 col = go * 4 + t
-                nc.scalar.activation(
-                    out=mid[:, t * UNIT : (t + 1) * UNIT],
-                    in_=acc[:],
-                    func=ACT.Identity,
-                    bias=bias[:, col : col + 1],
-                    scale=1.0,
-                )
+                dst = mid[:, t * UNIT : (t + 1) * UNIT]
+                if engines[t] == "S":
+                    nc.scalar.activation(
+                        out=dst, in_=acc[:], func=ACT.Identity, bias=bias[:, col : col + 1], scale=1.0
+                    )
+                else:
+                    nc.vector.tensor_scalar(
+                        out=dst, in0=acc[:], scalar1=bias[:, col : col + 1], scalar2=None, op0=ALU.add
+                    )
             pgrp = midp.tile([P, 4 * UNIT], BF16, name="pgrp", align_bytes=64)
             nc.vector.tensor_copy(
                 out=pgrp[:].rearrange("p (c i t) -> p c t i", i=4, t=4),
                 in_=mid[:].rearrange("p (t c i) -> p c t i", t=4, i=4),
             )
+            nl = slice(go * UNIT, (go + 1) * UNIT)
             nc.vector.quantize_mx(
-                out=pj_op[h][0][:, go * UNIT : (go + 1) * UNIT].bitcast(FP8X4),
-                scales=pj_op[h][1][:, go * UNIT : (go + 1) * UNIT],
-                in_=pgrp[:],
+                out=pj_op[h][0][:, nl].bitcast(FP8X4), scales=pj_op[h][1][:, nl], in_=pgrp[:]
             )
 
         out_v = out.rearrange("(g p r) (c k) -> g c p r k", p=P, r=4, c=2)
 
-        def scores(op, sums, r, h):
+        def scores(g, op, sums, r, h):
             acc = psum.tile([P, UNIT], F32, name="acc", tag="mm")
-            mx_group(acc, op, r, pj_op[h])
+            mx_group(acc, op[0], op[1], r * P, pj_op[h][0], pj_op[h][1])
             scr = scrp.tile([P, UNIT], F32, name="scr")
             col = 2 * r + h
             nc.scalar.activation(
@@ -199,34 +192,47 @@ def tile_miscore_t_kernel(tc, y_a, y_b, W, b, out):
             for c in range(2):
                 nc.sync.dma_start(out=out_v[g][c][:, r, :], in_=ot[:, r * UNIT : (r + 1) * UNIT])
 
-        prepare(raw_yb0, yb_op[0], "SVSS", True, False, True)
-        prepare(raw_w0, w_op[0], "SVSS", False, True, True)
-        prepare(raw_w1, w_op[1], "SVSS", False, True, True)
-        stage1(0, 0)
-        prepare(raw_yb1, yb_op[1], "SVSS", True, True)
-        stage1(1, 0)
+        prepare(raw_yb[0], yb_op[0], "SVSS", True)
+        prepare(raw_w[0], w_op[0], "SVSS", True)
+        nc.vector.tensor_copy(out=bias[:], in_=b_raw[:])
+        prepare(raw_w[1], w_op[1], "SVSS", True)
+        stage1(0, 0, "SSSS")
+        prepare(raw_yb[1], yb_op[1], "SVSS")
+        stage1(1, 0, "SSSS")
         ya_op = operand(yacp, "ya")
-        prepare(raw_ya[0], ya_op, "SVSV", False, False)
-        stage1(0, 1)
-        stage1(1, 1)
+        prepare(raw_ya[0], ya_op, "SVSV")
+        stage1(0, 1, "SSSS")
+        stage1(1, 1, "SSSS")
+        late = None
         for g in range(GROUPS):
             sums = scrp.tile([P, 8], F32, name="sums", bufs=3)
             ot = outp.tile([P, 4 * UNIT], F32, name="ot")
             more = g + 1 < GROUPS
-            if g == 0:
+            if more:
                 next_op = operand(yacp, "ya")
-                prepare(raw_ya[1], next_op, "VVVV", False, True)
+                banks, grp = transposes(raw_ya[g + 1])
+                evacuate("V", banks, grp, 0)
+            if late is not None:
+                finish(*late)
+            if more:
+                for t in range(1, 4):
+                    evacuate("V", banks, grp, t)
+            if g == 0:
                 for h in range(2):
                     for r in range(4):
-                        scores(ya_op, sums, r, h)
-                        if h == 1:
-                            finish(g, sums, ot, r)
+                        scores(g, ya_op, sums, r, h)
+                quantise(grp, next_op)
+                for r in range(3):
+                    finish(g, sums, ot, r)
             else:
                 for r in range(4):
-                    if more and r == 4 - AHEAD:
-                        next_op = operand(yacp, "ya")
-                        prepare(raw_ya[g + 1], next_op, "VVVV", False, True)
                     for h in range(2):
-                        scores(ya_op, sums, r, h)
-                    finish(g, sums, ot, r)
-            ya_op = next_op
+                        scores(g, ya_op, sums, r, h)
+                    if r < 3:
+                        finish(g, sums, ot, r)
+                    if r == 0 and more:
+                        quantise(grp, next_op)
+            late = (g, sums, ot, 3)
+            if more:
+                ya_op = next_op
+        finish(*late)

from contextlib import ExitStack

import concourse.mybir as mybir
from concourse.masks import make_identity

F32 = mybir.dt.float32
BF16 = mybir.dt.bfloat16
U32 = mybir.dt.uint32
U8 = mybir.dt.uint8
FP8X4 = mybir.dt.float8_e4m3fn_x4
ACT = mybir.ActivationFunctionType
ALU = mybir.AluOpType

P = 128
K = 1024
UNIT = 512
NA = 4096
NB = 1024
GROUPS = NA // UNIT
WARM = 8

FLOPS = 2 * NB * K * K + 2 * NA * NB * K


def tile_miscore_t_kernel(tc, y_a, y_b, W, b, out):
    nc = tc.nc
    with ExitStack() as ctx:
        ctx.enter_context(tc.manual_schedule())
        const = ctx.enter_context(tc.tile_pool(name="const", bufs=1))
        rawp = ctx.enter_context(tc.tile_pool(name="rawp", bufs=1))
        grpp = ctx.enter_context(tc.tile_pool(name="grpp", bufs=3))
        midp = ctx.enter_context(tc.tile_pool(name="midp", bufs=2))
        keep = ctx.enter_context(tc.tile_pool(name="keep", bufs=1))
        yacp = ctx.enter_context(tc.tile_pool(name="yacp", bufs=3))
        outp = ctx.enter_context(tc.tile_pool(name="outp", bufs=3))
        scrp = ctx.enter_context(tc.tile_pool(name="scrp", bufs=2))
        psum = ctx.enter_context(tc.psum_pool(name="psum", bufs=4))

        ident = const.tile([P, P], F32, name="ident")
        make_identity(nc, ident[:])
        b_raw = const.tile([P, 8], BF16, name="b_raw")
        with nc.allow_non_contiguous_dma(reason="bias: 512 pieces of two elements, once"):
            nc.scalar.dma_start(
                out=b_raw[:].rearrange("p (a e) -> p a e", e=2),
                in_=b.rearrange("(a p e) -> p a e", p=P, e=2),
            )
        bias = const.tile([P, 8], F32, name="bias")
        warm = const.tile([P, 8], F32, name="warm")
        nc.vector.memset(warm[:, 0:1], 0.0)
        nc.scalar.activation(out=warm[:, 1:2], in_=warm[:, 0:1], func=ACT.Sigmoid)

        zl = const.tile([P, P], BF16, name="zl")
        zr = const.tile([P, UNIT], BF16, name="zr")
        nc.vector.memset(zl[:], 0.0)
        nc.vector.memset(zr[:], 0.0)

        def idle_matmuls(n):
            for i in range(n):
                junk = psum.tile([P, UNIT], F32, name="junk", tag="mm")
                nc.tensor.matmul(out=junk[:], lhsT=zl[:], rhs=zr[:], start=True, stop=True)

        idle_matmuls(WARM)

        ya_v = y_a.rearrange("(g p r) k -> g p r k", p=P, r=4)
        yb_v = y_b.rearrange("(g p r) k -> g p r k", p=P, r=4)
        w_v = W.rearrange("(g u p e) k -> g u p e k", u=2, p=P, e=2)

        def load(name, halves):
            raw = rawp.tile([P, 4 * K], BF16, name=name)
            n = len(halves)
            for i, src in enumerate(halves):
                w = 4 * K // n
                nc.sync.dma_start(
                    out=raw[:, i * w : (i + 1) * w].rearrange("p (r k) -> p r k", k=K), in_=src
                )
            return raw

        raw_yb = [None, None]
        raw_w = [None, None]
        raw_yb[0] = load("raw_yb0", [yb_v[0][:, 0:2, :], yb_v[0][:, 2:4, :]])
        raw_w[0] = load("raw_w0", [w_v[0][0], w_v[0][1]])
        raw_w[1] = load("raw_w1", [w_v[1][0], w_v[1][1]])
        raw_yb[1] = load("raw_yb1", [yb_v[1][:, 0:2, :], yb_v[1][:, 2:4, :]])
        raw_ya = [load("raw_ya%d" % g, [ya_v[g]]) for g in range(GROUPS)]

        def copy_on(which, dst, src):
            if which == "S":
                nc.scalar.copy(out=dst, in_=src)
            else:
                nc.vector.tensor_copy(out=dst, in_=src)

        def transposes(raw, fill=False):
            words = raw[:].bitcast(F32)
            banks = []
            for t in range(4):
                xt = psum.tile([P, 4, P], F32, name="xt", tag="tp")
                for c in range(4):
                    lo = t * (K // 2) + c * P
                    nc.tensor.transpose(xt[:, c, :], words[:, lo : lo + P], ident[:])
                banks.append(xt)
                if fill and t % 2 == 1:
                    idle_matmuls(1)
            grp = grpp.tile([P, 4 * K], BF16, name="grp", align_bytes=64)
            return banks, grp

        def evacuate(which, banks, grp, t):
            gw = grp[:].bitcast(F32).rearrange("p (g c u) -> p g c u", g=2, u=2)
            copy_on(
                which,
                gw[:, :, t * P : (t + 1) * P, :],
                banks[t][:].rearrange("p (g u) i -> p g i u", g=2),
            )

        def quantise(grp, op):
            nc.vector.quantize_mx(out=op[0][:].bitcast(FP8X4), scales=op[1][:], in_=grp[:])

        def prepare(raw, op, engines, fill=False):
            banks, grp = transposes(raw, fill)
            for t in range(4):
                evacuate(engines[t], banks, grp, t)
            quantise(grp, op)

        def operand(pool, name):
            codes = pool.tile([P, 2 * UNIT], U32, name=name + "_c", align_bytes=64)
            scales = pool.tile([P, 2 * UNIT], U8, name=name + "_s", align_bytes=64)
            return codes, scales

        def mx_group(acc, lc, ls, m0, rc, rs):
            for gk in range(2):
                ml = slice(gk * UNIT + m0, gk * UNIT + m0 + P)
                nl = slice(gk * UNIT, (gk + 1) * UNIT)
                nc.tensor.matmul_mx(
                    out=acc[:],
                    lhsT=lc[:, ml].bitcast(FP8X4),
                    lhsT_scale=ls[:, ml],
                    rhs=rc[:, nl].bitcast(FP8X4),
                    rhs_scale=rs[:, nl],
                    start=(gk == 0),
                    stop=(gk == 1),
                )

        yb_op = [operand(keep, "yb%d" % h) for h in range(2)]
        w_op = [operand(keep, "w%d" % g) for g in range(2)]
        pj_op = [operand(keep, "pj%d" % h) for h in range(2)]

        def stage1(go, h, engines):
            mid = midp.tile([P, 4 * UNIT], BF16, name="mid")
            for t in range(4):
                acc = psum.tile([P, UNIT], F32, name="acc", tag="mm")
                mx_group(acc, w_op[go][0], w_op[go][1], t * P, yb_op[h][0], yb_op[h][1])
                col = go * 4 + t
                dst = mid[:, t * UNIT : (t + 1) * UNIT]
                if engines[t] == "S":
                    nc.scalar.activation(
                        out=dst, in_=acc[:], func=ACT.Identity, bias=bias[:, col : col + 1], scale=1.0
                    )
                else:
                    nc.vector.tensor_scalar(
                        out=dst, in0=acc[:], scalar1=bias[:, col : col + 1], scalar2=None, op0=ALU.add
                    )
            pgrp = midp.tile([P, 4 * UNIT], BF16, name="pgrp", align_bytes=64)
            nc.vector.tensor_copy(
                out=pgrp[:].rearrange("p (c i t) -> p c t i", i=4, t=4),
                in_=mid[:].rearrange("p (t c i) -> p c t i", t=4, i=4),
            )
            nl = slice(go * UNIT, (go + 1) * UNIT)
            nc.vector.quantize_mx(
                out=pj_op[h][0][:, nl].bitcast(FP8X4), scales=pj_op[h][1][:, nl], in_=pgrp[:]
            )

        out_v = out.rearrange("(g p r) (c k) -> g c p r k", p=P, r=4, c=2)

        def scores(g, op, sums, r, h):
            acc = psum.tile([P, UNIT], F32, name="acc", tag="mm")
            mx_group(acc, op[0], op[1], r * P, pj_op[h][0], pj_op[h][1])
            scr = scrp.tile([P, UNIT], F32, name="scr")
            col = 2 * r + h
            nc.scalar.activation(
                out=scr[:], in_=acc[:], func=ACT.Sigmoid, accum_out=sums[:, col : col + 1]
            )

        def finish(g, sums, ot, r):
            filler = nc.vector if g == GROUPS - 1 else nc.gpsimd
            filler.tensor_scalar(
                out=ot[:, r * UNIT : (r + 1) * UNIT],
                in0=sums[:, 2 * r : 2 * r + 1].to_broadcast([P, UNIT]),
                scalar1=sums[:, 2 * r + 1 : 2 * r + 2],
                scalar2=1.0 / K,
                op0=ALU.add,
                op1=ALU.mult,
            )
            for c in range(2):
                nc.sync.dma_start(out=out_v[g][c][:, r, :], in_=ot[:, r * UNIT : (r + 1) * UNIT])

        prepare(raw_yb[0], yb_op[0], "SVSS", True)
        prepare(raw_w[0], w_op[0], "SVSS", True)
        nc.vector.tensor_copy(out=bias[:], in_=b_raw[:])
        prepare(raw_w[1], w_op[1], "SVSS", True)
        stage1(0, 0, "SSSS")
        prepare(raw_yb[1], yb_op[1], "SVSS")
        stage1(1, 0, "SSSS")
        ya_op = operand(yacp, "ya")
        prepare(raw_ya[0], ya_op, "SVSV")
        stage1(0, 1, "SSSS")
        stage1(1, 1, "SSSS")
        late = None
        for g in range(GROUPS):
            sums = scrp.tile([P, 8], F32, name="sums", bufs=3)
            ot = outp.tile([P, 4 * UNIT], F32, name="ot")
            more = g + 1 < GROUPS
            if more:
                next_op = operand(yacp, "ya")
                banks, grp = transposes(raw_ya[g + 1])
                evacuate("V", banks, grp, 0)
            if late is not None:
                finish(*late)
            if more:
                for t in range(1, 4):
                    evacuate("V", banks, grp, t)
            if g == 0:
                for h in range(2):
                    for r in range(4):
                        scores(g, ya_op, sums, r, h)
                quantise(grp, next_op)
                for r in range(3):
                    finish(g, sums, ot, r)
            else:
                for r in range(4):
                    for h in range(2):
                        scores(g, ya_op, sums, r, h)
                    if r < 3:
                        finish(g, sums, ot, r)
                    if r == 0 and more:
                        quantise(grp, next_op)
            late = (g, sums, ot, 3)
            if more:
                ya_op = next_op
        finish(*late)
